import numpy as np
import ml_dtypes


def mxq(x, axis, fmt="e4m3"):
    dtype, down = {"e4m3": (ml_dtypes.float8_e4m3fn, 7), "e5m2": (ml_dtypes.float8_e5m2, 14)}[fmt]
    v = np.moveaxis(np.asarray(x, np.float32).astype(ml_dtypes.bfloat16).astype(np.float64), axis, -1)
    blocks = v.reshape(v.shape[:-1] + (-1, 32))
    amax = np.abs(blocks).max(-1, keepdims=True)
    byte = np.maximum(np.where(amax > 0, np.frexp(amax)[1] - 1 + 127, 0) - down, 1)
    scale = np.exp2(byte - 127.0)
    codes = (blocks / scale).astype(np.float32).astype(dtype).astype(np.float64)
    return np.moveaxis((codes * scale).reshape(v.shape), -1, axis)


WIDE = False


def mx_kscale(k):
    if not WIDE:
        return np.ones(k)
    levels = np.array([10, -10, 5, -5, 0])
    a = np.random.permutation(np.resize(levels, k // 512 * 4)).reshape(k // 512, 4)
    idx = np.arange(k)
    return np.exp2(a[idx // 512, idx % 128 // 32])


BF16 = ml_dtypes.bfloat16


def bf(x):
    return np.asarray(x, np.float32).astype(BF16)


def f64(x):
    return np.asarray(x).astype(np.float64)


B, T, D, F, LNS = 64, 40, 512, 2048, 8


def erf(z):
    a = np.minimum(np.abs(z), 6.0)
    d = 2.0 * a * a
    term = a.copy()
    total = a.copy()
    n = 0
    while np.any(term > 1e-18 * total):
        n += 1
        term = term * d / (2 * n + 1)
        total = total + term
    return np.sign(z) * np.minimum(2.0 / np.sqrt(np.pi) * np.exp(-a * a) * total, 1.0)


def gelu(v):
    return 0.5 * v * (1.0 + erf(v / np.sqrt(2.0)))


def setup_inputs():
    s = mx_kscale(D)
    return {"x_tail": bf(np.random.standard_normal((B, LNS, D)) * s),
            "W1NS": bf(np.random.standard_normal((LNS, D, F)) / np.sqrt(D) / s[None, :, None]),
            "W2NS": bf(np.random.standard_normal((LNS, F, D)) / np.sqrt(F))}


def reference(x_tail, W1NS, W2NS):
    xp = f64(x_tail).transpose(1, 0, 2)
    h = gelu(mxq(xp, 2, "e4m3") @ mxq(f64(W1NS), 1, "e4m3"))
    y = mxq(h, 2, "e4m3") @ mxq(f64(W2NS), 1, "e4m3")
    return y.transpose(1, 0, 2)

@@ -1,0 +1,266 @@
+from contextlib import ExitStack
+
+import concourse.mybir as mybir
+from concourse.masks import make_identity
+
+FLOPS = 2 * 2 * 64 * 8 * 512 * 2048
+
+BF16 = mybir.dt.bfloat16
+F32 = mybir.dt.float32
+I32 = mybir.dt.int32
+U32 = mybir.dt.uint32
+U8 = mybir.dt.uint8
+FP8X4 = mybir.dt.float8_e4m3fn_x4
+GELU = mybir.ActivationFunctionType.Gelu
+
+P = 128
+B = 64
+T = 8
+D = 512
+F = 2048
+RAW_BUFS = 6
+V_SHARE_A = 72
+V_SHARE_B = 72
+
+
+def tile_mixedffn_pa_kernel(tc, x_tail, W1NS, W2NS, out):
+    nc = tc.nc
+    with ExitStack() as ctx:
+        const = ctx.enter_context(tc.tile_pool(name="const", bufs=1))
+        rawp = ctx.enter_context(tc.tile_pool(name="rawp", bufs=RAW_BUFS))
+        piecep = ctx.enter_context(tc.tile_pool(name="piecep", bufs=4))
+        grpp = ctx.enter_context(tc.tile_pool(name="grpp", bufs=4))
+        codp = ctx.enter_context(tc.tile_pool(name="codp", bufs=5))
+        hgp = ctx.enter_context(tc.tile_pool(name="hgp", bufs=2))
+        yp = ctx.enter_context(tc.tile_pool(name="yp", bufs=3))
+        ps_x = ctx.enter_context(tc.psum_pool(name="ps_x", bufs=2))
+        ps_a = ctx.enter_context(tc.psum_pool(name="ps_a", bufs=3))
+        ps_y = ctx.enter_context(tc.psum_pool(name="ps_y", bufs=2))
+        ctx.enter_context(tc.manual_schedule())
+
+        order = [("A", 0), ("A", 1)]
+        for t in range(T - 2):
+            order.append(("B", t))
+            order.append(("A", t + 2))
+        order.append(("B", T - 2))
+        order.append(("B", T - 1))
+
+        items = []
+        loads = []
+        for n, (kind, t) in enumerate(order):
+            if n == 0 or n == len(order) - 1:
+                for g in range(4):
+                    loads.append({"kind": kind, "t": t, "g": g, "whole": False})
+                    items.append({"kind": kind, "t": t, "gs": [g], "load": len(loads) - 1, "last": False})
+            else:
+                loads.append({"kind": kind, "t": t, "g": None, "whole": True})
+                items.append({"kind": kind, "t": t, "gs": [0, 1], "load": len(loads) - 1, "last": False})
+                items.append({"kind": kind, "t": t, "gs": [2, 3], "load": len(loads) - 1, "last": True})
+        n_items = len(items)
+        state = {"next_load": 0, "whole_live": 0}
+        tiles = {}
+
+        def issue_load(i):
+            ld = loads[i]
+            w = W1NS if ld["kind"] == "A" else W2NS
+            t = ld["t"]
+            if ld["whole"]:
+                raw = rawp.tile([P, 8192], BF16, name="raw", tag="raw")
+                if ld["kind"] == "A":
+                    nc.sync.dma_start(out=raw[:, :], in_=w[t].rearrange("(p j) f -> p (j f)", j=4))
+                else:
+                    nc.sync.dma_start(
+                        out=raw[:, :].rearrange("p (g r) -> p g r", g=4),
+                        in_=w[t].rearrange("(g p j) d -> p g (j d)", g=4, p=P, j=4),
+                    )
+            else:
+                g = ld["g"]
+                raw = piecep.tile([P, 2048], BF16, name="piece", tag="piece")
+                if ld["kind"] == "A":
+                    nc.sync.dma_start(
+                        out=raw[:, :].rearrange("p (j f) -> p j f", j=4),
+                        in_=w[t][:, 512 * g : 512 * (g + 1)].rearrange("(p j) f -> p j f", j=4),
+                    )
+                else:
+                    nc.sync.dma_start(
+                        out=raw[:, :],
+                        in_=w[t][512 * g : 512 * (g + 1), :].rearrange("(p j) d -> p (j d)", j=4),
+                    )
+            tiles[("raw", i)] = raw
+
+        def issue_loads():
+            while state["next_load"] < len(loads):
+                i = state["next_load"]
+                if loads[i]["whole"] and state["whole_live"] >= RAW_BUFS:
+                    return
+                if (not loads[i]["whole"]) and i >= 4 and state["whole_live"] >= RAW_BUFS:
+                    return
+                issue_load(i)
+                if loads[i]["whole"]:
+                    state["whole_live"] += 1
+                state["next_load"] += 1
+                if i == 0:
+                    nc.sync.dma_start(
+                        out=x_sb[:, :].rearrange("r (q d) -> r q d", q=4),
+                        in_=x_tail.rearrange("b t d -> (b t) d").rearrange("(q r) d -> r q d", r=P),
+                    )
+
+        x_sb = const.tile([P, 4 * D], BF16, name="x_sb")
+        gx = const.tile([P, T * B * 4], BF16, name="gx", align_bytes=64)
+        xc = const.tile([P, T * B], U32, name="xc", align_bytes=64)
+        xs = const.tile([P, T * B], U8, name="xs", align_bytes=64)
+        ident = const.tile([P, P], F32, name="ident")
+        warm_in = const.tile([P, 8], F32, name="warm_in")
+        warm_out = const.tile([P, 8], F32, name="warm_out")
+        hc = [const.tile([P, 320], U32, name="hc%d" % i, align_bytes=64) for i in range(2)]
+        hs = [const.tile([P, 320], U8, name="hs%d" % i, align_bytes=64) for i in range(2)]
+
+        issue_loads()
+        make_identity(nc, ident[:, :])
+        nc.vector.memset(warm_in[:, :], 0.0)
+        nc.scalar.activation(out=warm_out[:, :], in_=warm_in[:, :], func=GELU)
+        for i in range(2):
+            nc.vector.memset(hc[i][:, :].bitcast(I32), 0)
+            nc.vector.memset(hs[i][:, :].bitcast(I32), 0)
+
+        xw = x_sb[:, :].bitcast(F32).rearrange("r (q p u) -> r q u p", q=4, p=P, u=2)
+        gxw = gx[:, :].bitcast(F32).rearrange("p (t b u) -> p t b u", t=T, b=B, u=2)
+        xts = []
+        for h in range(2):
+            xt = ps_x.tile([P, 512], F32, name="xt", tag="xt")
+            for u in range(2):
+                for ql in range(2):
+                    nc.tensor.transpose(
+                        xt[:, u * 256 + ql * P : u * 256 + (ql + 1) * P], xw[:, 2 * h + ql, u, :], ident[:, :]
+                    )
+            xts.append(xt)
+
+        def x_copy_out():
+            for h in range(2):
+                dst = gxw[:, :, 32 * h : 32 * (h + 1), :]
+                src = xts[h][:, :].rearrange("p (u b t) -> p t b u", u=2, b=32, t=T)
+                if h == 0:
+                    nc.vector.tensor_copy(out=dst, in_=src)
+                else:
+                    nc.scalar.copy(out=dst, in_=src)
+
+        def x_quantise():
+            nc.vector.quantize_mx(out=xc[:, :].bitcast(FP8X4), scales=xs[:, :], in_=gx[:, :])
+
+        def regroup(i):
+            it = items[i]
+            ng = len(it["gs"])
+            raw = tiles[("raw", it["load"])]
+            grp = grpp.tile([P, 4096], BF16, name="grp", tag="grp", align_bytes=64)
+            tiles[("grp", i)] = grp
+            if it["kind"] == "A":
+                share = V_SHARE_A
+                spat = "p (t g c i) -> p g c t i"
+                dpat = "p (g i c t) -> p g c t i"
+            else:
+                share = V_SHARE_B
+                spat = "p (g t c i) -> p g c t i"
+                dpat = "p (g c i t) -> p g c t i"
+            if loads[it["load"]]["whole"]:
+                src = raw[:, :].rearrange(spat, g=4, t=4, c=P, i=4)[:, it["gs"][0] : it["gs"][0] + ng]
+            else:
+                src = raw[:, :].rearrange(spat, g=1, t=4, c=P, i=4)
+            dst = grp[:, 0 : 2048 * ng].rearrange(dpat, g=ng, t=4, c=P, i=4)
+            if ng == 1:
+                nc.vector.tensor_copy(out=dst[:, 0, 0:share], in_=src[:, 0, 0:share])
+            else:
+                nc.vector.tensor_copy(out=dst[:, :, 0:share], in_=src[:, :, 0:share])
+            for gi in range(ng):
+                nc.scalar.copy(out=dst[:, gi, share:P], in_=src[:, gi, share:P])
+            if it["last"]:
+                state["whole_live"] -= 1
+                issue_loads()
+
+        def quantise(i):
+            it = items[i]
+            w = 512 * len(it["gs"])
+            codes = codp.tile([P, 1024], U32, name="codes", tag="codes", align_bytes=64)
+            scales = codp.tile([P, 1024], U8, name="scales", tag="scales", align_bytes=64)
+            tiles[("codes", i)] = codes
+            tiles[("scales", i)] = scales
+            nc.vector.quantize_mx(
+                out=codes[:, 0:w].bitcast(FP8X4), scales=scales[:, 0:w], in_=tiles[("grp", i)][:, 0 : 4 * w]
+            )
+
+        def multiply(i):
+            it = items[i]
+            t = it["t"]
+            codes = tiles[("codes", i)]
+            scales = tiles[("scales", i)]
+            if it["kind"] == "A":
+                acc = ps_a.tile([P, 512], F32, name="acc_a", tag="acc_a")
+                tiles[("acc_a", i)] = acc
+                for col in range(4 * len(it["gs"])):
+                    nc.tensor.matmul_mx(
+                        out=acc[:, col * B : (col + 1) * B],
+                        lhsT=codes[:, col * P : (col + 1) * P].bitcast(FP8X4),
+                        lhsT_scale=scales[:, col * P : (col + 1) * P],
+                        rhs=xc[:, t * B : (t + 1) * B].bitcast(FP8X4),
+                        rhs_scale=xs[:, t * B : (t + 1) * B],
+                        start=True,
+                        stop=True,
+                    )
+            else:
+                if it["gs"][0] == 0:
+                    acc_y = ps_y.tile([P, 512], F32, name="acc_y", tag="acc_y")
+                    tiles[("acc_y", t)] = acc_y
+                acc = tiles[("acc_y", t)]
+                for gi, g in enumerate(it["gs"]):
+                    nc.tensor.matmul_mx(
+                        out=acc[:, :],
+                        lhsT=hc[t % 2][:, B * g : B * g + P].bitcast(FP8X4),
+                        lhsT_scale=hs[t % 2][:, B * g : B * g + P],
+                        rhs=codes[:, gi * 512 : (gi + 1) * 512].bitcast(FP8X4),
+                        rhs_scale=scales[:, gi * 512 : (gi + 1) * 512],
+                        start=(g == 0),
+                        stop=(g == 3),
+                    )
+
+        def finish(i):
+            it = items[i]
+            t = it["t"]
+            ng = len(it["gs"])
+            if it["kind"] == "A":
+                if it["gs"][0] == 0:
+                    hg_new = hgp.tile([P, 1024], BF16, name="hg", tag="hg", align_bytes=64)
+                    tiles[("hg", t)] = hg_new
+                hg = tiles[("hg", t)]
+                g0 = it["gs"][0]
+                nc.scalar.activation(
+                    out=hg[:, 256 * g0 : 256 * (g0 + ng)].rearrange("p (g b j) -> p g b j", g=ng, b=B, j=4),
+                    in_=tiles[("acc_a", i)][:, 0 : 256 * ng].rearrange("p (g j b) -> p g b j", g=ng, j=4, b=B),
+                    func=GELU,
+                )
+            elif it["gs"][-1] == 3:
+                y = yp.tile([P, 512], F32, name="y", tag="y")
+                nc.scalar.copy(out=y[0:B, :], in_=tiles[("acc_y", t)][0:B, :])
+                nc.scalar.dma_start(out=out[:, t, :], in_=y[0:B, :])
+
+        def quantise_h(i):
+            it = items[i]
+            t = it["t"]
+            if it["kind"] == "A" and it["gs"][-1] == 3:
+                nc.vector.quantize_mx(
+                    out=hc[t % 2][:, 0:256].bitcast(FP8X4), scales=hs[t % 2][:, 0:256], in_=tiles[("hg", t)][:, :]
+                )
+
+        for s in range(n_items + 4):
+            if s < n_items:
+                regroup(s)
+            if s == 0:
+                x_copy_out()
+            if 0 <= s - 1 < n_items:
+                quantise(s - 1)
+            if s == 1:
+                x_quantise()
+            if 0 <= s - 4 < n_items:
+                quantise_h(s - 4)
+            if 0 <= s - 2 < n_items:
+                multiply(s - 2)
+            if 0 <= s - 3 < n_items:
+                finish(s - 3)

@@ -19,8 +19,8 @@ T = 8
 D = 512
 F = 2048
 RAW_BUFS = 6
-V_SHARE_A = 72
-V_SHARE_B = 72
+V_SHARE_A = 68
+V_SHARE_B = 68
 
 
 def tile_mixedffn_pa_kernel(tc, x_tail, W1NS, W2NS, out):

@@ -19,8 +19,9 @@ T = 8
 D = 512
 F = 2048
 RAW_BUFS = 6
-V_SHARE_A = 68
-V_SHARE_B = 68
+V_SHARE_A = 72
+V_SHARE_B = 72
+PERMUTED = ()
 
 
 def tile_mixedffn_pa_kernel(tc, x_tail, W1NS, W2NS, out):
@@ -68,10 +69,15 @@ def tile_mixedffn_pa_kernel(tc, x_tail, W1NS, W2NS, out):
                 raw = rawp.tile([P, 8192], BF16, name="raw", tag="raw")
                 if ld["kind"] == "A":
                     nc.sync.dma_start(out=raw[:, :], in_=w[t].rearrange("(p j) f -> p (j f)", j=4))
-                else:
+                elif t in PERMUTED:
                     nc.sync.dma_start(
                         out=raw[:, :].rearrange("p (g r) -> p g r", g=4),
                         in_=w[t].rearrange("(g p j) d -> p g (j d)", g=4, p=P, j=4),
+                    )
+                else:
+                    nc.sync.dma_start(
+                        out=raw[:, :].rearrange("p (r d) -> p r d", r=16),
+                        in_=w[t].rearrange("(r p) d -> p r d", r=16, p=P),
                     )
             else:
                 g = ld["g"]
@@ -81,10 +87,15 @@ def tile_mixedffn_pa_kernel(tc, x_tail, W1NS, W2NS, out):
                         out=raw[:, :].rearrange("p (j f) -> p j f", j=4),
                         in_=w[t][:, 512 * g : 512 * (g + 1)].rearrange("(p j) f -> p j f", j=4),
                     )
-                else:
+                elif t in PERMUTED:
                     nc.sync.dma_start(
                         out=raw[:, :],
                         in_=w[t][512 * g : 512 * (g + 1), :].rearrange("(p j) d -> p (j d)", j=4),
+                    )
+                else:
+                    nc.sync.dma_start(
+                        out=raw[:, :].rearrange("p (j d) -> p j d", j=4),
+                        in_=w[t][512 * g : 512 * (g + 1), :].rearrange("(j p) d -> p j d", j=4, p=P),
                     )
             tiles[("raw", i)] = raw
 
@@ -156,7 +167,7 @@ def tile_mixedffn_pa_kernel(tc, x_tail, W1NS, W2NS, out):
             if it["kind"] == "A":
                 share = V_SHARE_A
                 spat = "p (t g c i) -> p g c t i"
-                dpat = "p (g i c t) -> p g c t i"
+                dpat = "p (g i c t) -> p g c t i" if it["t"] in PERMUTED else "p (g c i t) -> p g c t i"
             else:
                 share = V_SHARE_B
                 spat = "p (g t c i) -> p g c t i"

@@ -18,17 +18,17 @@ B = 64
 T = 8
 D = 512
 F = 2048
-RAW_BUFS = 6
+HALF_BUFS = 10
 V_SHARE_A = 72
-V_SHARE_B = 72
-PERMUTED = ()
+V_SHARE_B = 70
+X_STEP = 2
 
 
 def tile_mixedffn_pa_kernel(tc, x_tail, W1NS, W2NS, out):
     nc = tc.nc
     with ExitStack() as ctx:
         const = ctx.enter_context(tc.tile_pool(name="const", bufs=1))
-        rawp = ctx.enter_context(tc.tile_pool(name="rawp", bufs=RAW_BUFS))
+        halfp = ctx.enter_context(tc.tile_pool(name="halfp", bufs=HALF_BUFS))
         piecep = ctx.enter_context(tc.tile_pool(name="piecep", bufs=4))
         grpp = ctx.enter_context(tc.tile_pool(name="grpp", bufs=4))
         codp = ctx.enter_context(tc.tile_pool(name="codp", bufs=5))
@@ -47,68 +47,47 @@ def tile_mixedffn_pa_kernel(tc, x_tail, W1NS, W2NS, out):
         order.append(("B", T - 1))
 
         items = []
-        loads = []
         for n, (kind, t) in enumerate(order):
             if n == 0 or n == len(order) - 1:
                 for g in range(4):
-                    loads.append({"kind": kind, "t": t, "g": g, "whole": False})
-                    items.append({"kind": kind, "t": t, "gs": [g], "load": len(loads) - 1, "last": False})
+                    items.append({"kind": kind, "t": t, "gs": [g]})
             else:
-                loads.append({"kind": kind, "t": t, "g": None, "whole": True})
-                items.append({"kind": kind, "t": t, "gs": [0, 1], "load": len(loads) - 1, "last": False})
-                items.append({"kind": kind, "t": t, "gs": [2, 3], "load": len(loads) - 1, "last": True})
+                items.append({"kind": kind, "t": t, "gs": [0, 1]})
+                items.append({"kind": kind, "t": t, "gs": [2, 3]})
         n_items = len(items)
-        state = {"next_load": 0, "whole_live": 0}
+        n_halves = n_items - 8
+        state = {"next_load": 0}
         tiles = {}
 
         def issue_load(i):
-            ld = loads[i]
-            w = W1NS if ld["kind"] == "A" else W2NS
-            t = ld["t"]
-            if ld["whole"]:
-                raw = rawp.tile([P, 8192], BF16, name="raw", tag="raw")
-                if ld["kind"] == "A":
-                    nc.sync.dma_start(out=raw[:, :], in_=w[t].rearrange("(p j) f -> p (j f)", j=4))
-                elif t in PERMUTED:
-                    nc.sync.dma_start(
-                        out=raw[:, :].rearrange("p (g r) -> p g r", g=4),
-                        in_=w[t].rearrange("(g p j) d -> p g (j d)", g=4, p=P, j=4),
-                    )
-                else:
-                    nc.sync.dma_start(
-                        out=raw[:, :].rearrange("p (r d) -> p r d", r=16),
-                        in_=w[t].rearrange("(r p) d -> p r d", r=16, p=P),
-                    )
+            it = items[i]
+            t = it["t"]
+            g0 = it["gs"][0]
+            ng = len(it["gs"])
+            if ng == 2:
+                raw = halfp.tile([P, 4096], BF16, name="half", tag="half")
             else:
-                g = ld["g"]
                 raw = piecep.tile([P, 2048], BF16, name="piece", tag="piece")
-                if ld["kind"] == "A":
-                    nc.sync.dma_start(
-                        out=raw[:, :].rearrange("p (j f) -> p j f", j=4),
-                        in_=w[t][:, 512 * g : 512 * (g + 1)].rearrange("(p j) f -> p j f", j=4),
-                    )
-                elif t in PERMUTED:
-                    nc.sync.dma_start(
-                        out=raw[:, :],
-                        in_=w[t][512 * g : 512 * (g + 1), :].rearrange("(p j) d -> p (j d)", j=4),
-                    )
-                else:
-                    nc.sync.dma_start(
-                        out=raw[:, :].rearrange("p (j d) -> p j d", j=4),
-                        in_=w[t][512 * g : 512 * (g + 1), :].rearrange("(j p) d -> p j d", j=4, p=P),
-                    )
+            if it["kind"] == "A":
+                nc.sync.dma_start(
+                    out=raw[:, :].rearrange("p (j f) -> p j f", j=4),
+                    in_=W1NS[t][:, 512 * g0 : 512 * (g0 + ng)].rearrange("(p j) f -> p j f", j=4),
+                )
+            else:
+                nc.sync.dma_start(
+                    out=raw[:, :].rearrange("p (g r) -> p g r", g=ng),
+                    in_=W2NS[t][512 * g0 : 512 * (g0 + ng), :].rearrange("(g p j) d -> p g (j d)", g=ng, p=P, j=4),
+                )
             tiles[("raw", i)] = raw
 
-        def issue_loads():
-            while state["next_load"] < len(loads):
+        def issue_loads(consumed):
+            while state["next_load"] < n_items:
                 i = state["next_load"]
-                if loads[i]["whole"] and state["whole_live"] >= RAW_BUFS:
+                if 4 <= i < 4 + n_halves and i - HALF_BUFS >= 4 and i - HALF_BUFS > consumed:
                     return
-                if (not loads[i]["whole"]) and i >= 4 and state["whole_live"] >= RAW_BUFS:
+                if i >= 4 + n_halves and consumed < 3:
                     return
                 issue_load(i)
-                if loads[i]["whole"]:
-                    state["whole_live"] += 1
                 state["next_load"] += 1
                 if i == 0:
                     nc.sync.dma_start(
@@ -126,7 +105,7 @@ def tile_mixedffn_pa_kernel(tc, x_tail, W1NS, W2NS, out):
         hc = [const.tile([P, 320], U32, name="hc%d" % i, align_bytes=64) for i in range(2)]
         hs = [const.tile([P, 320], U8, name="hs%d" % i, align_bytes=64) for i in range(2)]
 
-        issue_loads()
+        issue_loads(-1)
         make_identity(nc, ident[:, :])
         nc.vector.memset(warm_in[:, :], 0.0)
         nc.scalar.activation(out=warm_out[:, :], in_=warm_in[:, :], func=GELU)
@@ -161,21 +140,18 @@ def tile_mixedffn_pa_kernel(tc, x_tail, W1NS, W2NS, out):
         def regroup(i):
             it = items[i]
             ng = len(it["gs"])
-            raw = tiles[("raw", it["load"])]
+            raw = tiles[("raw", i)]
             grp = grpp.tile([P, 4096], BF16, name="grp", tag="grp", align_bytes=64)
             tiles[("grp", i)] = grp
             if it["kind"] == "A":
                 share = V_SHARE_A
                 spat = "p (t g c i) -> p g c t i"
-                dpat = "p (g i c t) -> p g c t i" if it["t"] in PERMUTED else "p (g c i t) -> p g c t i"
+                dpat = "p (g i c t) -> p g c t i"
             else:
                 share = V_SHARE_B
                 spat = "p (g t c i) -> p g c t i"
                 dpat = "p (g c i t) -> p g c t i"
-            if loads[it["load"]]["whole"]:
-                src = raw[:, :].rearrange(spat, g=4, t=4, c=P, i=4)[:, it["gs"][0] : it["gs"][0] + ng]
-            else:
-                src = raw[:, :].rearrange(spat, g=1, t=4, c=P, i=4)
+            src = raw[:, :].rearrange(spat, g=ng, t=4, c=P, i=4)
             dst = grp[:, 0 : 2048 * ng].rearrange(dpat, g=ng, t=4, c=P, i=4)
             if ng == 1:
                 nc.vector.tensor_copy(out=dst[:, 0, 0:share], in_=src[:, 0, 0:share])
@@ -183,9 +159,7 @@ def tile_mixedffn_pa_kernel(tc, x_tail, W1NS, W2NS, out):
                 nc.vector.tensor_copy(out=dst[:, :, 0:share], in_=src[:, :, 0:share])
             for gi in range(ng):
                 nc.scalar.copy(out=dst[:, gi, share:P], in_=src[:, gi, share:P])
-            if it["last"]:
-                state["whole_live"] -= 1
-                issue_loads()
+            issue_loads(i)
 
         def quantise(i):
             it = items[i]
@@ -250,7 +224,7 @@ def tile_mixedffn_pa_kernel(tc, x_tail, W1NS, W2NS, out):
             elif it["gs"][-1] == 3:
                 y = yp.tile([P, 512], F32, name="y", tag="y")
                 nc.scalar.copy(out=y[0:B, :], in_=tiles[("acc_y", t)][0:B, :])
-                nc.scalar.dma_start(out=out[:, t, :], in_=y[0:B, :])
+                nc.sync.dma_start(out=out[:, t, :], in_=y[0:B, :])
 
         def quantise_h(i):
             it = items[i]
@@ -263,15 +237,18 @@ def tile_mixedffn_pa_kernel(tc, x_tail, W1NS, W2NS, out):
         for s in range(n_items + 4):
             if s < n_items:
                 regroup(s)
-            if s == 0:
+            if s == X_STEP:
                 x_copy_out()
             if 0 <= s - 1 < n_items:
                 quantise(s - 1)
-            if s == 1:
+            if s == X_STEP + 1:
                 x_quantise()
-            if 0 <= s - 4 < n_items:
-                quantise_h(s - 4)
-            if 0 <= s - 2 < n_items:
-                multiply(s - 2)
-            if 0 <= s - 3 < n_items:
-                finish(s - 3)
+            for i in range(n_items):
+                if max(i + 4, X_STEP + 3) == s:
+                    quantise_h(i)
+            for i in range(n_items):
+                if max(i + 2, X_STEP + 1) == s:
+                    multiply(i)
+            for i in range(n_items):
+                if max(i + 3, X_STEP + 2) == s:
+                    finish(i)

@@ -22,6 +22,7 @@ HALF_BUFS = 10
 V_SHARE_A = 72
 V_SHARE_B = 70
 X_STEP = 2
+TAIL_GROUPS = [(0, 256), (256, 384), (384, 512)]
 
 
 def tile_mixedffn_pa_kernel(tc, x_tail, W1NS, W2NS, out):
@@ -33,7 +34,7 @@ def tile_mixedffn_pa_kernel(tc, x_tail, W1NS, W2NS, out):
         grpp = ctx.enter_context(tc.tile_pool(name="grpp", bufs=4))
         codp = ctx.enter_context(tc.tile_pool(name="codp", bufs=5))
         hgp = ctx.enter_context(tc.tile_pool(name="hgp", bufs=2))
-        yp = ctx.enter_context(tc.tile_pool(name="yp", bufs=3))
+        yp = ctx.enter_context(tc.tile_pool(name="yp", bufs=4))
         ps_x = ctx.enter_context(tc.psum_pool(name="ps_x", bufs=2))
         ps_a = ctx.enter_context(tc.psum_pool(name="ps_a", bufs=3))
         ps_y = ctx.enter_context(tc.psum_pool(name="ps_y", bufs=2))
@@ -46,21 +47,29 @@ def tile_mixedffn_pa_kernel(tc, x_tail, W1NS, W2NS, out):
         order.append(("B", T - 2))
         order.append(("B", T - 1))
 
+        loads = []
         items = []
         for n, (kind, t) in enumerate(order):
             if n == 0 or n == len(order) - 1:
                 for g in range(4):
-                    items.append({"kind": kind, "t": t, "gs": [g]})
+                    loads.append({"kind": kind, "t": t, "gs": [g]})
+                    if n > 0 and g == 3:
+                        for k, (d0, d1) in enumerate(TAIL_GROUPS):
+                            items.append({"kind": kind, "t": t, "gs": [g], "load": len(loads) - 1, "d0": d0, "d1": d1, "k": k})
+                    else:
+                        items.append({"kind": kind, "t": t, "gs": [g], "load": len(loads) - 1, "d0": 0, "d1": 512, "k": None})
             else:
-                items.append({"kind": kind, "t": t, "gs": [0, 1]})
-                items.append({"kind": kind, "t": t, "gs": [2, 3]})
+                for h in range(2):
+                    loads.append({"kind": kind, "t": t, "gs": [2 * h, 2 * h + 1]})
+                    items.append({"kind": kind, "t": t, "gs": [2 * h, 2 * h + 1], "load": len(loads) - 1, "d0": 0, "d1": 512, "k": None})
         n_items = len(items)
-        n_halves = n_items - 8
+        n_loads = len(loads)
+        n_halves = n_loads - 8
         state = {"next_load": 0}
         tiles = {}
 
         def issue_load(i):
-            it = items[i]
+            it = loads[i]
             t = it["t"]
             g0 = it["gs"][0]
             ng = len(it["gs"])
@@ -81,7 +90,7 @@ def tile_mixedffn_pa_kernel(tc, x_tail, W1NS, W2NS, out):
             tiles[("raw", i)] = raw
 
         def issue_loads(consumed):
-            while state["next_load"] < n_items:
+            while state["next_load"] < n_loads:
                 i = state["next_load"]
                 if 4 <= i < 4 + n_halves and i - HALF_BUFS >= 4 and i - HALF_BUFS > consumed:
                     return
@@ -140,7 +149,9 @@ def tile_mixedffn_pa_kernel(tc, x_tail, W1NS, W2NS, out):
         def regroup(i):
             it = items[i]
             ng = len(it["gs"])
-            raw = tiles[("raw", i)]
+            raw = tiles[("raw", it["load"])]
+            c0 = it["d0"] // 4
+            nc_cols = (it["d1"] - it["d0"]) // 4
             grp = grpp.tile([P, 4096], BF16, name="grp", tag="grp", align_bytes=64)
             tiles[("grp", i)] = grp
             if it["kind"] == "A":
@@ -151,19 +162,20 @@ def tile_mixedffn_pa_kernel(tc, x_tail, W1NS, W2NS, out):
                 share = V_SHARE_B
                 spat = "p (g t c i) -> p g c t i"
                 dpat = "p (g c i t) -> p g c t i"
-            src = raw[:, :].rearrange(spat, g=ng, t=4, c=P, i=4)
-            dst = grp[:, 0 : 2048 * ng].rearrange(dpat, g=ng, t=4, c=P, i=4)
+            share = 2 * ((share * nc_cols + P) // (2 * P))
+            src = raw[:, :].rearrange(spat, g=ng, t=4, c=P, i=4)[:, :, c0 : c0 + nc_cols]
+            dst = grp[:, 0 : 16 * nc_cols * ng].rearrange(dpat, g=ng, t=4, c=nc_cols, i=4)
             if ng == 1:
                 nc.vector.tensor_copy(out=dst[:, 0, 0:share], in_=src[:, 0, 0:share])
             else:
                 nc.vector.tensor_copy(out=dst[:, :, 0:share], in_=src[:, :, 0:share])
             for gi in range(ng):
-                nc.scalar.copy(out=dst[:, gi, share:P], in_=src[:, gi, share:P])
-            issue_loads(i)
+                nc.scalar.copy(out=dst[:, gi, share:nc_cols], in_=src[:, gi, share:nc_cols])
+            issue_loads(it["load"] if it["d1"] == 512 else it["load"] - 1)
 
         def quantise(i):
             it = items[i]
-            w = 512 * len(it["gs"])
+            w = (it["d1"] - it["d0"]) * len(it["gs"])
             codes = codp.tile([P, 1024], U32, name="codes", tag="codes", align_bytes=64)
             scales = codp.tile([P, 1024], U8, name="scales", tag="scales", align_bytes=64)
             tiles[("codes", i)] = codes
@@ -191,20 +203,27 @@ def tile_mixedffn_pa_kernel(tc, x_tail, W1NS, W2NS, out):
                         stop=True,
                     )
             else:
+                groups = TAIL_GROUPS if t == T - 1 else [(0, 512)]
                 if it["gs"][0] == 0:
-                    acc_y = ps_y.tile([P, 512], F32, name="acc_y", tag="acc_y")
-                    tiles[("acc_y", t)] = acc_y
-                acc = tiles[("acc_y", t)]
+                    for k in range(len(groups)):
+                        if k == 0:
+                            acc_y = ps_y.tile([P, 512], F32, name="acc_y", tag="acc_y")
+                        else:
+                            acc_y = ps_x.tile([P, 512], F32, name="xt", tag="xt")
+                        tiles[("acc_y", t, k)] = acc_y
                 for gi, g in enumerate(it["gs"]):
-                    nc.tensor.matmul_mx(
-                        out=acc[:, :],
-                        lhsT=hc[t % 2][:, B * g : B * g + P].bitcast(FP8X4),
-                        lhsT_scale=hs[t % 2][:, B * g : B * g + P],
-                        rhs=codes[:, gi * 512 : (gi + 1) * 512].bitcast(FP8X4),
-                        rhs_scale=scales[:, gi * 512 : (gi + 1) * 512],
-                        start=(g == 0),
-                        stop=(g == 3),
-                    )
+                    for k, (d0, d1) in enumerate(groups):
+                        if it["k"] is None or it["k"] == k:
+                            lo = gi * 512 + d0 - it["d0"]
+                            nc.tensor.matmul_mx(
+                                out=tiles[("acc_y", t, k)][:, 0 : d1 - d0],
+                                lhsT=hc[t % 2][:, B * g : B * g + P].bitcast(FP8X4),
+                                lhsT_scale=hs[t % 2][:, B * g : B * g + P],
+                                rhs=codes[:, lo : lo + d1 - d0].bitcast(FP8X4),
+                                rhs_scale=scales[:, lo : lo + d1 - d0],
+                                start=(g == 0),
+                                stop=(g == 3),
+                            )
 
         def finish(i):
             it = items[i]
@@ -222,9 +241,11 @@ def tile_mixedffn_pa_kernel(tc, x_tail, W1NS, W2NS, out):
                     func=GELU,
                 )
             elif it["gs"][-1] == 3:
+                k = 0 if it["k"] is None else it["k"]
+                w = it["d1"] - it["d0"]
                 y = yp.tile([P, 512], F32, name="y", tag="y")
-                nc.scalar.copy(out=y[0:B, :], in_=tiles[("acc_y", t)][0:B, :])
-                nc.sync.dma_start(out=out[:, t, :], in_=y[0:B, :])
+                nc.scalar.copy(out=y[0:B, 0:w], in_=tiles[("acc_y", t, k)][0:B, 0:w])
+                nc.sync.dma_start(out=out[:, t, it["d0"] : it["d1"]], in_=y[0:B, 0:w])
 
         def quantise_h(i):
             it = items[i]

@@ -14,245 +14,265 @@ FP8X4 = mybir.dt.float8_e4m3fn_x4
 GELU = mybir.ActivationFunctionType.Gelu
 
 P = 128
-B = 64
-T = 8
-D = 512
-F = 2048
+PACK = 4
+K_PASS = P * PACK
+ROWS = 64
+POSITIONS = 8
+QUARTERS = 4
+
 HALF_BUFS = 10
-V_SHARE_A = 72
-V_SHARE_B = 70
+V_SHARE_W1 = 72
+V_SHARE_W2 = 68
 X_STEP = 2
-TAIL_GROUPS = [(0, 256), (256, 384), (384, 512)]
+TAIL_SLICES = [(0, 256), (256, 384), (384, 512)]
+
+
+def weight_stream():
+    order = [("W1", 0), ("W1", 1)]
+    for t in range(POSITIONS - 2):
+        order.append(("W2", t))
+        order.append(("W1", t + 2))
+    order.append(("W2", POSITIONS - 2))
+    order.append(("W2", POSITIONS - 1))
+
+    loads = []
+    items = []
+    for n, (kind, t) in enumerate(order):
+        if n == 0 or n == len(order) - 1:
+            for g in range(QUARTERS):
+                loads.append({"kind": kind, "t": t, "gs": [g]})
+                if n > 0 and g == QUARTERS - 1:
+                    for n_slice, (d0, d1) in enumerate(TAIL_SLICES):
+                        items.append(
+                            {"kind": kind, "t": t, "gs": [g], "load": len(loads) - 1, "d0": d0, "d1": d1, "slice": n_slice}
+                        )
+                else:
+                    items.append({"kind": kind, "t": t, "gs": [g], "load": len(loads) - 1, "d0": 0, "d1": 512, "slice": None})
+        else:
+            for half in range(2):
+                gs = [2 * half, 2 * half + 1]
+                loads.append({"kind": kind, "t": t, "gs": gs})
+                items.append({"kind": kind, "t": t, "gs": gs, "load": len(loads) - 1, "d0": 0, "d1": 512, "slice": None})
+    return loads, items
 
 
 def tile_mixedffn_pa_kernel(tc, x_tail, W1NS, W2NS, out):
     nc = tc.nc
+    loads, items = weight_stream()
+    n_loads = len(loads)
+    n_items = len(items)
+    first_half = QUARTERS
+    first_tail = n_loads - QUARTERS
+
     with ExitStack() as ctx:
         const = ctx.enter_context(tc.tile_pool(name="const", bufs=1))
-        halfp = ctx.enter_context(tc.tile_pool(name="halfp", bufs=HALF_BUFS))
-        piecep = ctx.enter_context(tc.tile_pool(name="piecep", bufs=4))
-        grpp = ctx.enter_context(tc.tile_pool(name="grpp", bufs=4))
-        codp = ctx.enter_context(tc.tile_pool(name="codp", bufs=5))
-        hgp = ctx.enter_context(tc.tile_pool(name="hgp", bufs=2))
-        yp = ctx.enter_context(tc.tile_pool(name="yp", bufs=4))
-        ps_x = ctx.enter_context(tc.psum_pool(name="ps_x", bufs=2))
-        ps_a = ctx.enter_context(tc.psum_pool(name="ps_a", bufs=3))
-        ps_y = ctx.enter_context(tc.psum_pool(name="ps_y", bufs=2))
+        half_pool = ctx.enter_context(tc.tile_pool(name="half_pool", bufs=HALF_BUFS))
+        quarter_pool = ctx.enter_context(tc.tile_pool(name="quarter_pool", bufs=QUARTERS))
+        grouped_pool = ctx.enter_context(tc.tile_pool(name="grouped_pool", bufs=4))
+        mx_pool = ctx.enter_context(tc.tile_pool(name="mx_pool", bufs=5))
+        h_pool = ctx.enter_context(tc.tile_pool(name="h_pool", bufs=2))
+        y_pool = ctx.enter_context(tc.tile_pool(name="y_pool", bufs=4))
+        side_banks = ctx.enter_context(tc.psum_pool(name="side_banks", bufs=2))
+        h_banks = ctx.enter_context(tc.psum_pool(name="h_banks", bufs=3))
+        y_banks = ctx.enter_context(tc.psum_pool(name="y_banks", bufs=2))
         ctx.enter_context(tc.manual_schedule())
 
-        order = [("A", 0), ("A", 1)]
-        for t in range(T - 2):
-            order.append(("B", t))
-            order.append(("A", t + 2))
-        order.append(("B", T - 2))
-        order.append(("B", T - 1))
+        x_sb = const.tile([P, 4 * K_PASS], BF16, name="x_sb")
+        x_grouped = const.tile([P, POSITIONS * ROWS * PACK], BF16, name="x_grouped", align_bytes=64)
+        x_words = const.tile([P, POSITIONS * ROWS], U32, name="x_words", align_bytes=64)
+        x_scales = const.tile([P, POSITIONS * ROWS], U8, name="x_scales", align_bytes=64)
+        ident = const.tile([P, P], F32, name="ident")
+        warm_in = const.tile([P, 8], F32, name="warm_in")
+        warm_out = const.tile([P, 8], F32, name="warm_out")
+        h_width = (QUARTERS + 1) * ROWS
+        h_words = [const.tile([P, h_width], U32, name="h_words%d" % parity, align_bytes=64) for parity in range(2)]
+        h_scales = [const.tile([P, h_width], U8, name="h_scales%d" % parity, align_bytes=64) for parity in range(2)]
 
-        loads = []
-        items = []
-        for n, (kind, t) in enumerate(order):
-            if n == 0 or n == len(order) - 1:
-                for g in range(4):
-                    loads.append({"kind": kind, "t": t, "gs": [g]})
-                    if n > 0 and g == 3:
-                        for k, (d0, d1) in enumerate(TAIL_GROUPS):
-                            items.append({"kind": kind, "t": t, "gs": [g], "load": len(loads) - 1, "d0": d0, "d1": d1, "k": k})
-                    else:
-                        items.append({"kind": kind, "t": t, "gs": [g], "load": len(loads) - 1, "d0": 0, "d1": 512, "k": None})
-            else:
-                for h in range(2):
-                    loads.append({"kind": kind, "t": t, "gs": [2 * h, 2 * h + 1]})
-                    items.append({"kind": kind, "t": t, "gs": [2 * h, 2 * h + 1], "load": len(loads) - 1, "d0": 0, "d1": 512, "k": None})
-        n_items = len(items)
-        n_loads = len(loads)
-        n_halves = n_loads - 8
-        state = {"next_load": 0}
         tiles = {}
+        issued = {"loads": 0}
 
         def issue_load(i):
-            it = loads[i]
-            t = it["t"]
-            g0 = it["gs"][0]
-            ng = len(it["gs"])
+            ld = loads[i]
+            t = ld["t"]
+            g0 = ld["gs"][0]
+            ng = len(ld["gs"])
             if ng == 2:
-                raw = halfp.tile([P, 4096], BF16, name="half", tag="half")
+                raw = half_pool.tile([P, 2 * PACK * 512], BF16, name="half", tag="half")
             else:
-                raw = piecep.tile([P, 2048], BF16, name="piece", tag="piece")
-            if it["kind"] == "A":
+                raw = quarter_pool.tile([P, PACK * 512], BF16, name="quarter", tag="quarter")
+            if ld["kind"] == "W1":
                 nc.sync.dma_start(
-                    out=raw[:, :].rearrange("p (j f) -> p j f", j=4),
-                    in_=W1NS[t][:, 512 * g0 : 512 * (g0 + ng)].rearrange("(p j) f -> p j f", j=4),
+                    out=raw[:, :].rearrange("p (j f) -> p j f", j=PACK),
+                    in_=W1NS[t][:, 512 * g0 : 512 * (g0 + ng)].rearrange("(p j) f -> p j f", j=PACK),
                 )
             else:
                 nc.sync.dma_start(
                     out=raw[:, :].rearrange("p (g r) -> p g r", g=ng),
-                    in_=W2NS[t][512 * g0 : 512 * (g0 + ng), :].rearrange("(g p j) d -> p g (j d)", g=ng, p=P, j=4),
+                    in_=W2NS[t][K_PASS * g0 : K_PASS * (g0 + ng), :].rearrange("(g p j) d -> p g (j d)", g=ng, p=P, j=PACK),
                 )
             tiles[("raw", i)] = raw
 
-        def issue_loads(consumed):
-            while state["next_load"] < n_loads:
-                i = state["next_load"]
-                if 4 <= i < 4 + n_halves and i - HALF_BUFS >= 4 and i - HALF_BUFS > consumed:
+        def issue_loads(regrouped):
+            while issued["loads"] < n_loads:
+                i = issued["loads"]
+                if first_half + HALF_BUFS <= i < first_tail and i - HALF_BUFS > regrouped:
                     return
-                if i >= 4 + n_halves and consumed < 3:
+                if i >= first_tail and regrouped < first_half - 1:
                     return
                 issue_load(i)
-                state["next_load"] += 1
+                issued["loads"] += 1
                 if i == 0:
                     nc.sync.dma_start(
-                        out=x_sb[:, :].rearrange("r (q d) -> r q d", q=4),
-                        in_=x_tail.rearrange("b t d -> (b t) d").rearrange("(q r) d -> r q d", r=P),
+                        out=x_sb[:, :].rearrange("r (n d) -> r n d", n=4),
+                        in_=x_tail.rearrange("b t d -> (b t) d").rearrange("(n r) d -> r n d", r=P),
                     )
 
-        x_sb = const.tile([P, 4 * D], BF16, name="x_sb")
-        gx = const.tile([P, T * B * 4], BF16, name="gx", align_bytes=64)
-        xc = const.tile([P, T * B], U32, name="xc", align_bytes=64)
-        xs = const.tile([P, T * B], U8, name="xs", align_bytes=64)
-        ident = const.tile([P, P], F32, name="ident")
-        warm_in = const.tile([P, 8], F32, name="warm_in")
-        warm_out = const.tile([P, 8], F32, name="warm_out")
-        hc = [const.tile([P, 320], U32, name="hc%d" % i, align_bytes=64) for i in range(2)]
-        hs = [const.tile([P, 320], U8, name="hs%d" % i, align_bytes=64) for i in range(2)]
-
         issue_loads(-1)
+
         make_identity(nc, ident[:, :])
         nc.vector.memset(warm_in[:, :], 0.0)
         nc.scalar.activation(out=warm_out[:, :], in_=warm_in[:, :], func=GELU)
-        for i in range(2):
-            nc.vector.memset(hc[i][:, :].bitcast(I32), 0)
-            nc.vector.memset(hs[i][:, :].bitcast(I32), 0)
+        for parity in range(2):
+            nc.vector.memset(h_words[parity][:, :].bitcast(I32), 0)
+            nc.vector.memset(h_scales[parity][:, :].bitcast(I32), 0)
 
-        xw = x_sb[:, :].bitcast(F32).rearrange("r (q p u) -> r q u p", q=4, p=P, u=2)
-        gxw = gx[:, :].bitcast(F32).rearrange("p (t b u) -> p t b u", t=T, b=B, u=2)
-        xts = []
-        for h in range(2):
-            xt = ps_x.tile([P, 512], F32, name="xt", tag="xt")
+        x_pairs = x_sb[:, :].bitcast(F32).rearrange("r (n p u) -> r n u p", n=4, p=P, u=2)
+        x_banks = []
+        for side in range(2):
+            bank = side_banks.tile([P, 512], F32, name="side", tag="side")
             for u in range(2):
-                for ql in range(2):
+                for n in range(2):
                     nc.tensor.transpose(
-                        xt[:, u * 256 + ql * P : u * 256 + (ql + 1) * P], xw[:, 2 * h + ql, u, :], ident[:, :]
+                        bank[:, u * 256 + n * P : u * 256 + (n + 1) * P], x_pairs[:, 2 * side + n, u, :], ident[:, :]
                     )
-            xts.append(xt)
+            x_banks.append(bank)
 
         def x_copy_out():
-            for h in range(2):
-                dst = gxw[:, :, 32 * h : 32 * (h + 1), :]
-                src = xts[h][:, :].rearrange("p (u b t) -> p t b u", u=2, b=32, t=T)
-                if h == 0:
+            grouped_pairs = x_grouped[:, :].bitcast(F32).rearrange("p (t b u) -> p t b u", t=POSITIONS, b=ROWS, u=2)
+            for side in range(2):
+                dst = grouped_pairs[:, :, 32 * side : 32 * (side + 1), :]
+                src = x_banks[side][:, :].rearrange("p (u b t) -> p t b u", u=2, b=32, t=POSITIONS)
+                if side == 0:
                     nc.vector.tensor_copy(out=dst, in_=src)
                 else:
                     nc.scalar.copy(out=dst, in_=src)
 
         def x_quantise():
-            nc.vector.quantize_mx(out=xc[:, :].bitcast(FP8X4), scales=xs[:, :], in_=gx[:, :])
+            nc.vector.quantize_mx(out=x_words[:, :].bitcast(FP8X4), scales=x_scales[:, :], in_=x_grouped[:, :])
 
         def regroup(i):
             it = items[i]
             ng = len(it["gs"])
             raw = tiles[("raw", it["load"])]
             c0 = it["d0"] // 4
-            nc_cols = (it["d1"] - it["d0"]) // 4
-            grp = grpp.tile([P, 4096], BF16, name="grp", tag="grp", align_bytes=64)
-            tiles[("grp", i)] = grp
-            if it["kind"] == "A":
-                share = V_SHARE_A
-                spat = "p (t g c i) -> p g c t i"
-                dpat = "p (g i c t) -> p g c t i"
+            quads = (it["d1"] - it["d0"]) // 4
+            grouped = grouped_pool.tile([P, 2 * PACK * 512], BF16, name="grouped", tag="grouped", align_bytes=64)
+            tiles[("grouped", i)] = grouped
+            if it["kind"] == "W1":
+                share = V_SHARE_W1
+                src_order = "p (j g c e) -> p g c j e"
+                dst_order = "p (g e c j) -> p g c j e"
             else:
-                share = V_SHARE_B
-                spat = "p (g t c i) -> p g c t i"
-                dpat = "p (g c i t) -> p g c t i"
-            share = 2 * ((share * nc_cols + P) // (2 * P))
-            src = raw[:, :].rearrange(spat, g=ng, t=4, c=P, i=4)[:, :, c0 : c0 + nc_cols]
-            dst = grp[:, 0 : 16 * nc_cols * ng].rearrange(dpat, g=ng, t=4, c=nc_cols, i=4)
+                share = V_SHARE_W2
+                src_order = "p (g j c e) -> p g c j e"
+                dst_order = "p (g c e j) -> p g c j e"
+            share = 2 * ((share * quads + P) // (2 * P))
+            src = raw[:, :].rearrange(src_order, g=ng, j=PACK, c=P, e=4)[:, :, c0 : c0 + quads]
+            dst = grouped[:, 0 : 4 * PACK * quads * ng].rearrange(dst_order, g=ng, j=PACK, c=quads, e=4)
             if ng == 1:
                 nc.vector.tensor_copy(out=dst[:, 0, 0:share], in_=src[:, 0, 0:share])
+                nc.scalar.copy(out=dst[:, 0, share:quads], in_=src[:, 0, share:quads])
             else:
                 nc.vector.tensor_copy(out=dst[:, :, 0:share], in_=src[:, :, 0:share])
-            for gi in range(ng):
-                nc.scalar.copy(out=dst[:, gi, share:nc_cols], in_=src[:, gi, share:nc_cols])
+                nc.scalar.copy(out=dst[:, :, share:quads], in_=src[:, :, share:quads])
             issue_loads(it["load"] if it["d1"] == 512 else it["load"] - 1)
 
         def quantise(i):
             it = items[i]
-            w = (it["d1"] - it["d0"]) * len(it["gs"])
-            codes = codp.tile([P, 1024], U32, name="codes", tag="codes", align_bytes=64)
-            scales = codp.tile([P, 1024], U8, name="scales", tag="scales", align_bytes=64)
-            tiles[("codes", i)] = codes
+            width = (it["d1"] - it["d0"]) * len(it["gs"])
+            words = mx_pool.tile([P, 1024], U32, name="words", tag="words", align_bytes=64)
+            scales = mx_pool.tile([P, 1024], U8, name="scales", tag="scales", align_bytes=64)
+            tiles[("words", i)] = words
             tiles[("scales", i)] = scales
             nc.vector.quantize_mx(
-                out=codes[:, 0:w].bitcast(FP8X4), scales=scales[:, 0:w], in_=tiles[("grp", i)][:, 0 : 4 * w]
+                out=words[:, 0:width].bitcast(FP8X4),
+                scales=scales[:, 0:width],
+                in_=tiles[("grouped", i)][:, 0 : PACK * width],
             )
 
         def multiply(i):
             it = items[i]
             t = it["t"]
-            codes = tiles[("codes", i)]
+            words = tiles[("words", i)]
             scales = tiles[("scales", i)]
-            if it["kind"] == "A":
-                acc = ps_a.tile([P, 512], F32, name="acc_a", tag="acc_a")
-                tiles[("acc_a", i)] = acc
-                for col in range(4 * len(it["gs"])):
+            if it["kind"] == "W1":
+                bank = h_banks.tile([P, 512], F32, name="h_sums", tag="h_sums")
+                tiles[("h_sums", i)] = bank
+                for op in range(PACK * len(it["gs"])):
                     nc.tensor.matmul_mx(
-                        out=acc[:, col * B : (col + 1) * B],
-                        lhsT=codes[:, col * P : (col + 1) * P].bitcast(FP8X4),
-                        lhsT_scale=scales[:, col * P : (col + 1) * P],
-                        rhs=xc[:, t * B : (t + 1) * B].bitcast(FP8X4),
-                        rhs_scale=xs[:, t * B : (t + 1) * B],
+                        out=bank[:, op * ROWS : (op + 1) * ROWS],
+                        lhsT=words[:, op * P : (op + 1) * P].bitcast(FP8X4),
+                        lhsT_scale=scales[:, op * P : (op + 1) * P],
+                        rhs=x_words[:, t * ROWS : (t + 1) * ROWS].bitcast(FP8X4),
+                        rhs_scale=x_scales[:, t * ROWS : (t + 1) * ROWS],
                         start=True,
                         stop=True,
                     )
             else:
-                groups = TAIL_GROUPS if t == T - 1 else [(0, 512)]
+                slices = TAIL_SLICES if t == POSITIONS - 1 else [(0, 512)]
                 if it["gs"][0] == 0:
-                    for k in range(len(groups)):
-                        if k == 0:
-                            acc_y = ps_y.tile([P, 512], F32, name="acc_y", tag="acc_y")
+                    for n_slice in range(len(slices)):
+                        if n_slice == 0:
+                            bank = y_banks.tile([P, 512], F32, name="y_sums", tag="y_sums")
                         else:
-                            acc_y = ps_x.tile([P, 512], F32, name="xt", tag="xt")
-                        tiles[("acc_y", t, k)] = acc_y
+                            bank = side_banks.tile([P, 512], F32, name="side", tag="side")
+                        tiles[("y_sums", t, n_slice)] = bank
                 for gi, g in enumerate(it["gs"]):
-                    for k, (d0, d1) in enumerate(groups):
-                        if it["k"] is None or it["k"] == k:
+                    for n_slice, (d0, d1) in enumerate(slices):
+                        if it["slice"] is None or it["slice"] == n_slice:
                             lo = gi * 512 + d0 - it["d0"]
                             nc.tensor.matmul_mx(
-                                out=tiles[("acc_y", t, k)][:, 0 : d1 - d0],
-                                lhsT=hc[t % 2][:, B * g : B * g + P].bitcast(FP8X4),
-                                lhsT_scale=hs[t % 2][:, B * g : B * g + P],
-                                rhs=codes[:, lo : lo + d1 - d0].bitcast(FP8X4),
+                                out=tiles[("y_sums", t, n_slice)][:, 0 : d1 - d0],
+                                lhsT=h_words[t % 2][:, ROWS * g : ROWS * g + P].bitcast(FP8X4),
+                                lhsT_scale=h_scales[t % 2][:, ROWS * g : ROWS * g + P],
+                                rhs=words[:, lo : lo + d1 - d0].bitcast(FP8X4),
                                 rhs_scale=scales[:, lo : lo + d1 - d0],
                                 start=(g == 0),
-                                stop=(g == 3),
+                                stop=(g == QUARTERS - 1),
                             )
 
-        def finish(i):
+        def leave_psum(i):
             it = items[i]
             t = it["t"]
             ng = len(it["gs"])
-            if it["kind"] == "A":
+            if it["kind"] == "W1":
                 if it["gs"][0] == 0:
-                    hg_new = hgp.tile([P, 1024], BF16, name="hg", tag="hg", align_bytes=64)
-                    tiles[("hg", t)] = hg_new
-                hg = tiles[("hg", t)]
+                    h_new = h_pool.tile([P, QUARTERS * ROWS * PACK], BF16, name="h_grouped", tag="h_grouped", align_bytes=64)
+                    tiles[("h_grouped", t)] = h_new
                 g0 = it["gs"][0]
+                per_g = ROWS * PACK
                 nc.scalar.activation(
-                    out=hg[:, 256 * g0 : 256 * (g0 + ng)].rearrange("p (g b j) -> p g b j", g=ng, b=B, j=4),
-                    in_=tiles[("acc_a", i)][:, 0 : 256 * ng].rearrange("p (g j b) -> p g b j", g=ng, j=4, b=B),
+                    out=tiles[("h_grouped", t)][:, per_g * g0 : per_g * (g0 + ng)].rearrange(
+                        "p (g b j) -> p g b j", g=ng, b=ROWS, j=PACK
+                    ),
+                    in_=tiles[("h_sums", i)][:, 0 : per_g * ng].rearrange("p (g j b) -> p g b j", g=ng, j=PACK, b=ROWS),
                     func=GELU,
                 )
-            elif it["gs"][-1] == 3:
-                k = 0 if it["k"] is None else it["k"]
-                w = it["d1"] - it["d0"]
-                y = yp.tile([P, 512], F32, name="y", tag="y")
-                nc.scalar.copy(out=y[0:B, 0:w], in_=tiles[("acc_y", t, k)][0:B, 0:w])
-                nc.sync.dma_start(out=out[:, t, it["d0"] : it["d1"]], in_=y[0:B, 0:w])
+            elif it["gs"][-1] == QUARTERS - 1:
+                n_slice = 0 if it["slice"] is None else it["slice"]
+                width = it["d1"] - it["d0"]
+                y = y_pool.tile([P, 512], F32, name="y", tag="y")
+                nc.scalar.copy(out=y[0:ROWS, 0:width], in_=tiles[("y_sums", t, n_slice)][0:ROWS, 0:width])
+                nc.sync.dma_start(out=out[:, t, it["d0"] : it["d1"]], in_=y[0:ROWS, 0:width])
 
         def quantise_h(i):
             it = items[i]
             t = it["t"]
-            if it["kind"] == "A" and it["gs"][-1] == 3:
+            if it["kind"] == "W1" and it["gs"][-1] == QUARTERS - 1:
                 nc.vector.quantize_mx(
-                    out=hc[t % 2][:, 0:256].bitcast(FP8X4), scales=hs[t % 2][:, 0:256], in_=tiles[("hg", t)][:, :]
+                    out=h_words[t % 2][:, 0 : QUARTERS * ROWS].bitcast(FP8X4),
+                    scales=h_scales[t % 2][:, 0 : QUARTERS * ROWS],
+                    in_=tiles[("h_grouped", t)][:, :],
                 )
 
         for s in range(n_items + 4):
@@ -272,4 +292,4 @@ def tile_mixedffn_pa_kernel(tc, x_tail, W1NS, W2NS, out):
                     multiply(i)
             for i in range(n_items):
                 if max(i + 3, X_STEP + 2) == s:
-                    finish(i)
+                    leave_psum(i)

@@ -164,8 +164,10 @@ def tile_mixedffn_pa_kernel(tc, x_tail, W1NS, W2NS, out):
             it = items[i]
             ng = len(it["gs"])
             raw = tiles[("raw", it["load"])]
-            c0 = it["d0"] // 4
-            quads = (it["d1"] - it["d0"]) // 4
+            run = 4 if it["kind"] == "W1" else 8
+            c0 = it["d0"] // run
+            runs = (it["d1"] - it["d0"]) // run
+            whole = 512 // run
             grouped = grouped_pool.tile([P, 2 * PACK * 512], BF16, name="grouped", tag="grouped", align_bytes=64)
             tiles[("grouped", i)] = grouped
             if it["kind"] == "W1":
@@ -176,15 +178,15 @@ def tile_mixedffn_pa_kernel(tc, x_tail, W1NS, W2NS, out):
                 share = V_SHARE_W2
                 src_order = "p (g j c e) -> p g c j e"
                 dst_order = "p (g c e j) -> p g c j e"
-            share = 2 * ((share * quads + P) // (2 * P))
-            src = raw[:, :].rearrange(src_order, g=ng, j=PACK, c=P, e=4)[:, :, c0 : c0 + quads]
-            dst = grouped[:, 0 : 4 * PACK * quads * ng].rearrange(dst_order, g=ng, j=PACK, c=quads, e=4)
+            share = 2 * ((share * runs + P) // (2 * P))
+            src = raw[:, :].rearrange(src_order, g=ng, j=PACK, c=whole, e=run)[:, :, c0 : c0 + runs]
+            dst = grouped[:, 0 : run * PACK * runs * ng].rearrange(dst_order, g=ng, j=PACK, c=runs, e=run)
             if ng == 1:
                 nc.vector.tensor_copy(out=dst[:, 0, 0:share], in_=src[:, 0, 0:share])
-                nc.scalar.copy(out=dst[:, 0, share:quads], in_=src[:, 0, share:quads])
+                nc.scalar.copy(out=dst[:, 0, share:runs], in_=src[:, 0, share:runs])
             else:
                 nc.vector.tensor_copy(out=dst[:, :, 0:share], in_=src[:, :, 0:share])
-                nc.scalar.copy(out=dst[:, :, share:quads], in_=src[:, :, share:quads])
+                nc.scalar.copy(out=dst[:, :, share:runs], in_=src[:, :, share:runs])
             issue_loads(it["load"] if it["d1"] == 512 else it["load"] - 1)
 
         def quantise(i):

@@ -121,7 +121,7 @@ def tile_mixedffn_pa_kernel(tc, x_tail, W1NS, W2NS, out):
                     return
                 issue_load(i)
                 issued["loads"] += 1
-                if i == 0:
+                if i == 1:
                     nc.sync.dma_start(
                         out=x_sb[:, :].rearrange("r (n d) -> r n d", n=4),
                         in_=x_tail.rearrange("b t d -> (b t) d").rearrange("(n r) d -> r n d", r=P),
@@ -164,29 +164,27 @@ def tile_mixedffn_pa_kernel(tc, x_tail, W1NS, W2NS, out):
             it = items[i]
             ng = len(it["gs"])
             raw = tiles[("raw", it["load"])]
-            run = 4 if it["kind"] == "W1" else 8
-            c0 = it["d0"] // run
-            runs = (it["d1"] - it["d0"]) // run
-            whole = 512 // run
             grouped = grouped_pool.tile([P, 2 * PACK * 512], BF16, name="grouped", tag="grouped", align_bytes=64)
             tiles[("grouped", i)] = grouped
             if it["kind"] == "W1":
-                share = V_SHARE_W1
-                src_order = "p (j g c e) -> p g c j e"
-                dst_order = "p (g e c j) -> p g c j e"
+                octs = ng * 512 // 8
+                share = V_SHARE_W1 * octs // P
+                src = raw[:, :].rearrange("p (j c k e) -> p c j e k", j=PACK, k=2, e=4)
+                dst = grouped[:, 0 : PACK * 512 * ng].rearrange("p (e c k j) -> p c j e k", e=4, k=2, j=PACK)
+                nc.vector.tensor_copy(out=dst[:, 0:share], in_=src[:, 0:share])
+                nc.scalar.copy(out=dst[:, share:octs], in_=src[:, share:octs])
             else:
-                share = V_SHARE_W2
-                src_order = "p (g j c e) -> p g c j e"
-                dst_order = "p (g c e j) -> p g c j e"
-            share = 2 * ((share * runs + P) // (2 * P))
-            src = raw[:, :].rearrange(src_order, g=ng, j=PACK, c=whole, e=run)[:, :, c0 : c0 + runs]
-            dst = grouped[:, 0 : run * PACK * runs * ng].rearrange(dst_order, g=ng, j=PACK, c=runs, e=run)
-            if ng == 1:
-                nc.vector.tensor_copy(out=dst[:, 0, 0:share], in_=src[:, 0, 0:share])
-                nc.scalar.copy(out=dst[:, 0, share:runs], in_=src[:, 0, share:runs])
-            else:
-                nc.vector.tensor_copy(out=dst[:, :, 0:share], in_=src[:, :, 0:share])
-                nc.scalar.copy(out=dst[:, :, share:runs], in_=src[:, :, share:runs])
+                c0 = it["d0"] // 8
+                octs = (it["d1"] - it["d0"]) // 8
+                share = 2 * ((V_SHARE_W2 * octs + P) // (2 * P))
+                src = raw[:, :].rearrange("p (g j c e) -> p g c j e", g=ng, j=PACK, e=8)[:, :, c0 : c0 + octs]
+                dst = grouped[:, 0 : 8 * PACK * octs * ng].rearrange("p (g c e j) -> p g c j e", g=ng, e=8, j=PACK)
+                if ng == 1:
+                    nc.vector.tensor_copy(out=dst[:, 0, 0:share], in_=src[:, 0, 0:share])
+                    nc.scalar.copy(out=dst[:, 0, share:octs], in_=src[:, 0, share:octs])
+                else:
+                    nc.vector.tensor_copy(out=dst[:, :, 0:share], in_=src[:, :, 0:share])
+                    nc.scalar.copy(out=dst[:, :, share:octs], in_=src[:, :, share:octs])
             issue_loads(it["load"] if it["d1"] == 512 else it["load"] - 1)
 
         def quantise(i):
@@ -210,9 +208,11 @@ def tile_mixedffn_pa_kernel(tc, x_tail, W1NS, W2NS, out):
             if it["kind"] == "W1":
                 bank = h_banks.tile([P, 512], F32, name="h_sums", tag="h_sums")
                 tiles[("h_sums", i)] = bank
-                for op in range(PACK * len(it["gs"])):
+                ng = len(it["gs"])
+                for out_at in range(PACK * ng):
+                    op = (out_at % PACK) * ng + out_at // PACK
                     nc.tensor.matmul_mx(
-                        out=bank[:, op * ROWS : (op + 1) * ROWS],
+                        out=bank[:, out_at * ROWS : (out_at + 1) * ROWS],
                         lhsT=words[:, op * P : (op + 1) * P].bitcast(FP8X4),
                         lhsT_scale=scales[:, op * P : (op + 1) * P],
                         rhs=x_words[:, t * ROWS : (t + 1) * ROWS].bitcast(FP8X4),

@@ -21,8 +21,8 @@ POSITIONS = 8
 QUARTERS = 4
 
 HALF_BUFS = 10
-V_SHARE_W1 = 72
-V_SHARE_W2 = 68
+V_SHARE_W1 = 70
+V_SHARE_W2 = 66
 X_STEP = 2
 TAIL_SLICES = [(0, 256), (256, 384), (384, 512)]
 
@@ -176,7 +176,7 @@ def tile_mixedffn_pa_kernel(tc, x_tail, W1NS, W2NS, out):
             else:
                 c0 = it["d0"] // 8
                 octs = (it["d1"] - it["d0"]) // 8
-                share = 2 * ((V_SHARE_W2 * octs + P) // (2 * P))
+                share = V_SHARE_W2 * octs // P
                 src = raw[:, :].rearrange("p (g j c e) -> p g c j e", g=ng, j=PACK, e=8)[:, :, c0 : c0 + octs]
                 dst = grouped[:, 0 : 8 * PACK * octs * ng].rearrange("p (g c e j) -> p g c j e", g=ng, e=8, j=PACK)
                 if ng == 1:

@@ -23,16 +23,16 @@ QUARTERS = 4
 HALF_BUFS = 10
 V_SHARE_W1 = 70
 V_SHARE_W2 = 66
-X_STEP = 2
+X_STEP = 6
+X_LOAD = 5
 TAIL_SLICES = [(0, 256), (256, 384), (384, 512)]
 
 
 def weight_stream():
-    order = [("W1", 0), ("W1", 1)]
-    for t in range(POSITIONS - 2):
+    order = [("W2", 0), ("W1", 0), ("W1", 1)]
+    for t in range(1, POSITIONS - 1):
+        order.append(("W1", t + 1))
         order.append(("W2", t))
-        order.append(("W1", t + 2))
-    order.append(("W2", POSITIONS - 2))
     order.append(("W2", POSITIONS - 1))
 
     loads = []
@@ -69,9 +69,9 @@ def tile_mixedffn_pa_kernel(tc, x_tail, W1NS, W2NS, out):
         half_pool = ctx.enter_context(tc.tile_pool(name="half_pool", bufs=HALF_BUFS))
         quarter_pool = ctx.enter_context(tc.tile_pool(name="quarter_pool", bufs=QUARTERS))
         grouped_pool = ctx.enter_context(tc.tile_pool(name="grouped_pool", bufs=4))
-        mx_pool = ctx.enter_context(tc.tile_pool(name="mx_pool", bufs=5))
+        mx_pool = ctx.enter_context(tc.tile_pool(name="mx_pool", bufs=11))
         h_pool = ctx.enter_context(tc.tile_pool(name="h_pool", bufs=2))
-        y_pool = ctx.enter_context(tc.tile_pool(name="y_pool", bufs=4))
+        y_pool = ctx.enter_context(tc.tile_pool(name="y_pool", bufs=POSITIONS))
         side_banks = ctx.enter_context(tc.psum_pool(name="side_banks", bufs=2))
         h_banks = ctx.enter_context(tc.psum_pool(name="h_banks", bufs=3))
         y_banks = ctx.enter_context(tc.psum_pool(name="y_banks", bufs=2))
@@ -90,6 +90,7 @@ def tile_mixedffn_pa_kernel(tc, x_tail, W1NS, W2NS, out):
 
         tiles = {}
         issued = {"loads": 0}
+        stores = []
 
         def issue_load(i):
             ld = loads[i]
@@ -121,10 +122,9 @@ def tile_mixedffn_pa_kernel(tc, x_tail, W1NS, W2NS, out):
                     return
                 issue_load(i)
                 issued["loads"] += 1
-                if i == 1:
+                if i == X_LOAD:
                     nc.sync.dma_start(
-                        out=x_sb[:, :].rearrange("r (n d) -> r n d", n=4),
-                        in_=x_tail.rearrange("b t d -> (b t) d").rearrange("(n r) d -> r n d", r=P),
+                        out=x_sb[:, :], in_=x_tail.rearrange("b t d -> (b t) d").rearrange("(r n) d -> r (n d)", n=4)
                     )
 
         issue_loads(-1)
@@ -148,10 +148,10 @@ def tile_mixedffn_pa_kernel(tc, x_tail, W1NS, W2NS, out):
             x_banks.append(bank)
 
         def x_copy_out():
-            grouped_pairs = x_grouped[:, :].bitcast(F32).rearrange("p (t b u) -> p t b u", t=POSITIONS, b=ROWS, u=2)
+            grouped_pairs = x_grouped[:, :].bitcast(F32).rearrange("p (a n b u) -> p n a b u", a=2, n=4, b=ROWS, u=2)
             for side in range(2):
-                dst = grouped_pairs[:, :, 32 * side : 32 * (side + 1), :]
-                src = x_banks[side][:, :].rearrange("p (u b t) -> p t b u", u=2, b=32, t=POSITIONS)
+                dst = grouped_pairs[:, 2 * side : 2 * side + 2]
+                src = x_banks[side][:, :].rearrange("p (u n b a) -> p n a b u", u=2, n=2, b=ROWS, a=2)
                 if side == 0:
                     nc.vector.tensor_copy(out=dst, in_=src)
                 else:
@@ -265,7 +265,13 @@ def tile_mixedffn_pa_kernel(tc, x_tail, W1NS, W2NS, out):
                 width = it["d1"] - it["d0"]
                 y = y_pool.tile([P, 512], F32, name="y", tag="y")
                 nc.scalar.copy(out=y[0:ROWS, 0:width], in_=tiles[("y_sums", t, n_slice)][0:ROWS, 0:width])
-                nc.sync.dma_start(out=out[:, t, it["d0"] : it["d1"]], in_=y[0:ROWS, 0:width])
+                stores.append((out[:, t, it["d0"] : it["d1"]], y[0:ROWS, 0:width]))
+
+        def issue_stores():
+            if issued["loads"] == n_loads:
+                for dst, src in stores:
+                    nc.sync.dma_start(out=dst, in_=src)
+                stores.clear()
 
         def quantise_h(i):
             it = items[i]
@@ -277,21 +283,28 @@ def tile_mixedffn_pa_kernel(tc, x_tail, W1NS, W2NS, out):
                     in_=tiles[("h_grouped", t)][:, :],
                 )
 
+        n_first = QUARTERS
+        h0_step = n_first + 1 + 4
+
+        def multiply_step(i):
+            return h0_step + 1 if i < n_first else i + 2
+
         for s in range(n_items + 4):
+            if s == X_STEP:
+                quantise(s - 1)
+                x_copy_out()
             if s < n_items:
                 regroup(s)
             if s == X_STEP:
-                x_copy_out()
-            if 0 <= s - 1 < n_items:
-                quantise(s - 1)
-            if s == X_STEP + 1:
                 x_quantise()
+            elif 0 <= s - 1 < n_items:
+                quantise(s - 1)
+            if n_first <= s - 4 < n_items:
+                quantise_h(s - 4)
             for i in range(n_items):
-                if max(i + 4, X_STEP + 3) == s:
-                    quantise_h(i)
-            for i in range(n_items):
-                if max(i + 2, X_STEP + 1) == s:
+                if multiply_step(i) == s:
                     multiply(i)
             for i in range(n_items):
-                if max(i + 3, X_STEP + 2) == s:
+                if multiply_step(i) + 1 == s:
                     leave_psum(i)
+            issue_stores()

@@ -21,7 +21,7 @@ POSITIONS = 8
 QUARTERS = 4
 
 HALF_BUFS = 10
-V_SHARE_W1 = 70
+V_SHARE_W1 = 72
 V_SHARE_W2 = 66
 X_STEP = 6
 X_LOAD = 5

from contextlib import ExitStack

import concourse.mybir as mybir
from concourse.masks import make_identity

FLOPS = 2 * 2 * 64 * 8 * 512 * 2048

BF16 = mybir.dt.bfloat16
F32 = mybir.dt.float32
I32 = mybir.dt.int32
U32 = mybir.dt.uint32
U8 = mybir.dt.uint8
FP8X4 = mybir.dt.float8_e4m3fn_x4
GELU = mybir.ActivationFunctionType.Gelu

P = 128
PACK = 4
K_PASS = P * PACK
ROWS = 64
POSITIONS = 8
QUARTERS = 4

HALF_BUFS = 10
V_SHARE_W1 = 72
V_SHARE_W2 = 66
X_STEP = 6
X_LOAD = 5
TAIL_SLICES = [(0, 256), (256, 384), (384, 512)]


def weight_stream():
    order = [("W2", 0), ("W1", 0), ("W1", 1)]
    for t in range(1, POSITIONS - 1):
        order.append(("W1", t + 1))
        order.append(("W2", t))
    order.append(("W2", POSITIONS - 1))

    loads = []
    items = []
    for n, (kind, t) in enumerate(order):
        if n == 0 or n == len(order) - 1:
            for g in range(QUARTERS):
                loads.append({"kind": kind, "t": t, "gs": [g]})
                if n > 0 and g == QUARTERS - 1:
                    for n_slice, (d0, d1) in enumerate(TAIL_SLICES):
                        items.append(
                            {"kind": kind, "t": t, "gs": [g], "load": len(loads) - 1, "d0": d0, "d1": d1, "slice": n_slice}
                        )
                else:
                    items.append({"kind": kind, "t": t, "gs": [g], "load": len(loads) - 1, "d0": 0, "d1": 512, "slice": None})
        else:
            for half in range(2):
                gs = [2 * half, 2 * half + 1]
                loads.append({"kind": kind, "t": t, "gs": gs})
                items.append({"kind": kind, "t": t, "gs": gs, "load": len(loads) - 1, "d0": 0, "d1": 512, "slice": None})
    return loads, items


def tile_mixedffn_pa_kernel(tc, x_tail, W1NS, W2NS, out):
    nc = tc.nc
    loads, items = weight_stream()
    n_loads = len(loads)
    n_items = len(items)
    first_half = QUARTERS
    first_tail = n_loads - QUARTERS

    with ExitStack() as ctx:
        const = ctx.enter_context(tc.tile_pool(name="const", bufs=1))
        half_pool = ctx.enter_context(tc.tile_pool(name="half_pool", bufs=HALF_BUFS))
        quarter_pool = ctx.enter_context(tc.tile_pool(name="quarter_pool", bufs=QUARTERS))
        grouped_pool = ctx.enter_context(tc.tile_pool(name="grouped_pool", bufs=4))
        mx_pool = ctx.enter_context(tc.tile_pool(name="mx_pool", bufs=11))
        h_pool = ctx.enter_context(tc.tile_pool(name="h_pool", bufs=2))
        y_pool = ctx.enter_context(tc.tile_pool(name="y_pool", bufs=POSITIONS))
        side_banks = ctx.enter_context(tc.psum_pool(name="side_banks", bufs=2))
        h_banks = ctx.enter_context(tc.psum_pool(name="h_banks", bufs=3))
        y_banks = ctx.enter_context(tc.psum_pool(name="y_banks", bufs=2))
        ctx.enter_context(tc.manual_schedule())

        x_sb = const.tile([P, 4 * K_PASS], BF16, name="x_sb")
        x_grouped = const.tile([P, POSITIONS * ROWS * PACK], BF16, name="x_grouped", align_bytes=64)
        x_words = const.tile([P, POSITIONS * ROWS], U32, name="x_words", align_bytes=64)
        x_scales = const.tile([P, POSITIONS * ROWS], U8, name="x_scales", align_bytes=64)
        ident = const.tile([P, P], F32, name="ident")
        warm_in = const.tile([P, 8], F32, name="warm_in")
        warm_out = const.tile([P, 8], F32, name="warm_out")
        h_width = (QUARTERS + 1) * ROWS
        h_words = [const.tile([P, h_width], U32, name="h_words%d" % parity, align_bytes=64) for parity in range(2)]
        h_scales = [const.tile([P, h_width], U8, name="h_scales%d" % parity, align_bytes=64) for parity in range(2)]

        tiles = {}
        issued = {"loads": 0}
        stores = []

        def issue_load(i):
            ld = loads[i]
            t = ld["t"]
            g0 = ld["gs"][0]
            ng = len(ld["gs"])
            if ng == 2:
                raw = half_pool.tile([P, 2 * PACK * 512], BF16, name="half", tag="half")
            else:
                raw = quarter_pool.tile([P, PACK * 512], BF16, name="quarter", tag="quarter")
            if ld["kind"] == "W1":
                nc.sync.dma_start(
                    out=raw[:, :].rearrange("p (j f) -> p j f", j=PACK),
                    in_=W1NS[t][:, 512 * g0 : 512 * (g0 + ng)].rearrange("(p j) f -> p j f", j=PACK),
                )
            else:
                nc.sync.dma_start(
                    out=raw[:, :].rearrange("p (g r) -> p g r", g=ng),
                    in_=W2NS[t][K_PASS * g0 : K_PASS * (g0 + ng), :].rearrange("(g p j) d -> p g (j d)", g=ng, p=P, j=PACK),
                )
            tiles[("raw", i)] = raw

        def issue_loads(regrouped):
            while issued["loads"] < n_loads:
                i = issued["loads"]
                if first_half + HALF_BUFS <= i < first_tail and i - HALF_BUFS > regrouped:
                    return
                if i >= first_tail and regrouped < first_half - 1:
                    return
                issue_load(i)
                issued["loads"] += 1
                if i == X_LOAD:
                    nc.sync.dma_start(
                        out=x_sb[:, :], in_=x_tail.rearrange("b t d -> (b t) d").rearrange("(r n) d -> r (n d)", n=4)
                    )

        issue_loads(-1)

        make_identity(nc, ident[:, :])
        nc.vector.memset(warm_in[:, :], 0.0)
        nc.scalar.activation(out=warm_out[:, :], in_=warm_in[:, :], func=GELU)
        for parity in range(2):
            nc.vector.memset(h_words[parity][:, :].bitcast(I32), 0)
            nc.vector.memset(h_scales[parity][:, :].bitcast(I32), 0)

        x_pairs = x_sb[:, :].bitcast(F32).rearrange("r (n p u) -> r n u p", n=4, p=P, u=2)
        x_banks = []
        for side in range(2):
            bank = side_banks.tile([P, 512], F32, name="side", tag="side")
            for u in range(2):
                for n in range(2):
                    nc.tensor.transpose(
                        bank[:, u * 256 + n * P : u * 256 + (n + 1) * P], x_pairs[:, 2 * side + n, u, :], ident[:, :]
                    )
            x_banks.append(bank)

        def x_copy_out():
            grouped_pairs = x_grouped[:, :].bitcast(F32).rearrange("p (a n b u) -> p n a b u", a=2, n=4, b=ROWS, u=2)
            for side in range(2):
                dst = grouped_pairs[:, 2 * side : 2 * side + 2]
                src = x_banks[side][:, :].rearrange("p (u n b a) -> p n a b u", u=2, n=2, b=ROWS, a=2)
                if side == 0:
                    nc.vector.tensor_copy(out=dst, in_=src)
                else:
                    nc.scalar.copy(out=dst, in_=src)

        def x_quantise():
            nc.vector.quantize_mx(out=x_words[:, :].bitcast(FP8X4), scales=x_scales[:, :], in_=x_grouped[:, :])

        def regroup(i):
            it = items[i]
            ng = len(it["gs"])
            raw = tiles[("raw", it["load"])]
            grouped = grouped_pool.tile([P, 2 * PACK * 512], BF16, name="grouped", tag="grouped", align_bytes=64)
            tiles[("grouped", i)] = grouped
            if it["kind"] == "W1":
                octs = ng * 512 // 8
                share = V_SHARE_W1 * octs // P
                src = raw[:, :].rearrange("p (j c k e) -> p c j e k", j=PACK, k=2, e=4)
                dst = grouped[:, 0 : PACK * 512 * ng].rearrange("p (e c k j) -> p c j e k", e=4, k=2, j=PACK)
                nc.vector.tensor_copy(out=dst[:, 0:share], in_=src[:, 0:share])
                nc.scalar.copy(out=dst[:, share:octs], in_=src[:, share:octs])
            else:
                c0 = it["d0"] // 8
                octs = (it["d1"] - it["d0"]) // 8
                share = V_SHARE_W2 * octs // P
                src = raw[:, :].rearrange("p (g j c e) -> p g c j e", g=ng, j=PACK, e=8)[:, :, c0 : c0 + octs]
                dst = grouped[:, 0 : 8 * PACK * octs * ng].rearrange("p (g c e j) -> p g c j e", g=ng, e=8, j=PACK)
                if ng == 1:
                    nc.vector.tensor_copy(out=dst[:, 0, 0:share], in_=src[:, 0, 0:share])
                    nc.scalar.copy(out=dst[:, 0, share:octs], in_=src[:, 0, share:octs])
                else:
                    nc.vector.tensor_copy(out=dst[:, :, 0:share], in_=src[:, :, 0:share])
                    nc.scalar.copy(out=dst[:, :, share:octs], in_=src[:, :, share:octs])
            issue_loads(it["load"] if it["d1"] == 512 else it["load"] - 1)

        def quantise(i):
            it = items[i]
            width = (it["d1"] - it["d0"]) * len(it["gs"])
            words = mx_pool.tile([P, 1024], U32, name="words", tag="words", align_bytes=64)
            scales = mx_pool.tile([P, 1024], U8, name="scales", tag="scales", align_bytes=64)
            tiles[("words", i)] = words
            tiles[("scales", i)] = scales
            nc.vector.quantize_mx(
                out=words[:, 0:width].bitcast(FP8X4),
                scales=scales[:, 0:width],
                in_=tiles[("grouped", i)][:, 0 : PACK * width],
            )

        def multiply(i):
            it = items[i]
            t = it["t"]
            words = tiles[("words", i)]
            scales = tiles[("scales", i)]
            if it["kind"] == "W1":
                bank = h_banks.tile([P, 512], F32, name="h_sums", tag="h_sums")
                tiles[("h_sums", i)] = bank
                ng = len(it["gs"])
                for out_at in range(PACK * ng):
                    op = (out_at % PACK) * ng + out_at // PACK
                    nc.tensor.matmul_mx(
                        out=bank[:, out_at * ROWS : (out_at + 1) * ROWS],
                        lhsT=words[:, op * P : (op + 1) * P].bitcast(FP8X4),
                        lhsT_scale=scales[:, op * P : (op + 1) * P],
                        rhs=x_words[:, t * ROWS : (t + 1) * ROWS].bitcast(FP8X4),
                        rhs_scale=x_scales[:, t * ROWS : (t + 1) * ROWS],
                        start=True,
                        stop=True,
                    )
            else:
                slices = TAIL_SLICES if t == POSITIONS - 1 else [(0, 512)]
                if it["gs"][0] == 0:
                    for n_slice in range(len(slices)):
                        if n_slice == 0:
                            bank = y_banks.tile([P, 512], F32, name="y_sums", tag="y_sums")
                        else:
                            bank = side_banks.tile([P, 512], F32, name="side", tag="side")
                        tiles[("y_sums", t, n_slice)] = bank
                for gi, g in enumerate(it["gs"]):
                    for n_slice, (d0, d1) in enumerate(slices):
                        if it["slice"] is None or it["slice"] == n_slice:
                            lo = gi * 512 + d0 - it["d0"]
                            nc.tensor.matmul_mx(
                                out=tiles[("y_sums", t, n_slice)][:, 0 : d1 - d0],
                                lhsT=h_words[t % 2][:, ROWS * g : ROWS * g + P].bitcast(FP8X4),
                                lhsT_scale=h_scales[t % 2][:, ROWS * g : ROWS * g + P],
                                rhs=words[:, lo : lo + d1 - d0].bitcast(FP8X4),
                                rhs_scale=scales[:, lo : lo + d1 - d0],
                                start=(g == 0),
                                stop=(g == QUARTERS - 1),
                            )

        def leave_psum(i):
            it = items[i]
            t = it["t"]
            ng = len(it["gs"])
            if it["kind"] == "W1":
                if it["gs"][0] == 0:
                    h_new = h_pool.tile([P, QUARTERS * ROWS * PACK], BF16, name="h_grouped", tag="h_grouped", align_bytes=64)
                    tiles[("h_grouped", t)] = h_new
                g0 = it["gs"][0]
                per_g = ROWS * PACK
                nc.scalar.activation(
                    out=tiles[("h_grouped", t)][:, per_g * g0 : per_g * (g0 + ng)].rearrange(
                        "p (g b j) -> p g b j", g=ng, b=ROWS, j=PACK
                    ),
                    in_=tiles[("h_sums", i)][:, 0 : per_g * ng].rearrange("p (g j b) -> p g b j", g=ng, j=PACK, b=ROWS),
                    func=GELU,
                )
            elif it["gs"][-1] == QUARTERS - 1:
                n_slice = 0 if it["slice"] is None else it["slice"]
                width = it["d1"] - it["d0"]
                y = y_pool.tile([P, 512], F32, name="y", tag="y")
                nc.scalar.copy(out=y[0:ROWS, 0:width], in_=tiles[("y_sums", t, n_slice)][0:ROWS, 0:width])
                stores.append((out[:, t, it["d0"] : it["d1"]], y[0:ROWS, 0:width]))

        def issue_stores():
            if issued["loads"] == n_loads:
                for dst, src in stores:
                    nc.sync.dma_start(out=dst, in_=src)
                stores.clear()

        def quantise_h(i):
            it = items[i]
            t = it["t"]
            if it["kind"] == "W1" and it["gs"][-1] == QUARTERS - 1:
                nc.vector.quantize_mx(
                    out=h_words[t % 2][:, 0 : QUARTERS * ROWS].bitcast(FP8X4),
                    scales=h_scales[t % 2][:, 0 : QUARTERS * ROWS],
                    in_=tiles[("h_grouped", t)][:, :],
                )

        n_first = QUARTERS
        h0_step = n_first + 1 + 4

        def multiply_step(i):
            return h0_step + 1 if i < n_first else i + 2

        for s in range(n_items + 4):
            if s == X_STEP:
                quantise(s - 1)
                x_copy_out()
            if s < n_items:
                regroup(s)
            if s == X_STEP:
                x_quantise()
            elif 0 <= s - 1 < n_items:
                quantise(s - 1)
            if n_first <= s - 4 < n_items:
                quantise_h(s - 4)
            for i in range(n_items):
                if multiply_step(i) == s:
                    multiply(i)
            for i in range(n_items):
                if multiply_step(i) + 1 == s:
                    leave_psum(i)
            issue_stores()
